import numpy as np
import ml_dtypes

BF16 = ml_dtypes.bfloat16


def bf(x):
    return np.asarray(x, np.float32).astype(BF16)


def f32(x):
    return np.asarray(x, np.float32)


def f64(x):
    return np.asarray(x).astype(np.float64)


def striped(idx):
    return np.tile(idx.reshape(-1, 16).T, (8, 1))


V, D, HID, N, RUN, K = 1024, 512, 1536, 1024, 512, 2
EPS = 1e-6
THRESH = 0.05
FFN_GAIN = 0.025
NORM_GAIN = 0.1


def ternary(shape):
    t = np.random.standard_normal(shape)
    return bf(np.sign(t) * (np.abs(t) > THRESH * np.abs(t).mean()))


def silu(v):
    return v / (1.0 + np.exp(-v))


def rms(x, gain):
    return x / np.sqrt(np.mean(x * x, axis=0, keepdims=True) + EPS) * gain


def setup_inputs():
    return {
        "emb": f32(np.random.standard_normal((D, V))),
        "rd": bf(np.random.uniform(size=(V, N))),
        "resid_w": bf(np.random.standard_normal((V, D)) * np.sqrt(3.0 / V)),
        "ffn_gain": f32(FFN_GAIN * (1.0 + 0.1 * np.random.standard_normal((D, 1)))),
        "w_gate": ternary((D, HID)),
        "w_up": ternary((D, HID)),
        "w_down": ternary((HID, D)),
        "norm_gain": f32(NORM_GAIN * (1.0 + 0.1 * np.random.standard_normal((D, 1)))),
        "head_w": ternary((D, V)),
        "offs": striped(np.concatenate([np.random.permutation(V)[:RUN] for _ in range(K)])),
    }


def reference(emb, rd, resid_w, ffn_gain, w_gate, w_up, w_down, norm_gain, head_w, offs):
    idx = offs[:16].T.reshape(-1)
    x0 = f64(emb)[:, idx] + f64(resid_w).T @ f64(rd)
    h = rms(x0, f64(ffn_gain))
    a = silu(f64(w_gate).T @ h) * (f64(w_up).T @ h)
    x1 = x0 + f64(w_down).T @ a
    y = rms(x1, f64(norm_gain))
    return f64(head_w).T @ y

@@ -1,0 +1,142 @@
+import concourse.mybir as mybir
+
+F32 = mybir.dt.float32
+BF16 = mybir.dt.bfloat16
+U16 = mybir.dt.uint16
+ACT = mybir.ActivationFunctionType
+ALU = mybir.AluOpType
+
+P = 128
+V, D, HID, N = 1024, 512, 1536, 1024
+EPS = 1e-6
+NH = 512
+HALVES = N // NH
+VB, CB, IB = V // P, D // P, HID // P
+WCOLS = 512
+WB = WCOLS // P
+WLOADS = HID // WCOLS
+
+FLOPS = 2 * N * (V * D + 2 * D * HID + HID * D + D * V)
+
+
+def tile_residualbitnettransformer_b_kernel(
+    tc, emb, rd, resid_w, ffn_gain, w_gate, w_up, w_down, norm_gain, head_w, offs, out
+):
+    nc = tc.nc
+    with (
+        tc.tile_pool(name="held", bufs=1) as held,
+        tc.tile_pool(name="work", bufs=4) as work,
+        tc.psum_pool(name="acc", bufs=6) as acc,
+        tc.psum_pool(name="stat", bufs=2) as stat,
+    ):
+        rd_sb = [[held.tile([P, NH], BF16, name=f"rd{h}_{k}") for k in range(VB)] for h in range(HALVES)]
+        rw_sb = [held.tile([P, D], BF16, name=f"rw{k}") for k in range(VB)]
+        emb_sb = [held.tile([P, V], F32, name=f"emb{c}") for c in range(CB)]
+        for k in range(VB):
+            nc.sync.dma_start(rd_sb[0][k][:], rd[k * P : (k + 1) * P, 0:NH])
+            nc.scalar.dma_start(rw_sb[k][:], resid_w[k * P : (k + 1) * P, :])
+        offsets = held.tile([P, N // 16], U16, name="offsets")
+        nc.sync.dma_start(offsets[:], offs)
+        gain1 = held.tile([P, CB], F32, name="gain1")
+        gain2 = held.tile([P, CB], F32, name="gain2")
+        nc.scalar.dma_start(gain1[:], ffn_gain.rearrange("(a p) o -> p (a o)", p=P))
+        nc.scalar.dma_start(gain2[:], norm_gain.rearrange("(a p) o -> p (a o)", p=P))
+        for c in range(CB):
+            nc.sync.dma_start(emb_sb[c][:], emb[c * P : (c + 1) * P, :])
+            for k in (2 * c, 2 * c + 1):
+                nc.sync.dma_start(rd_sb[1][k][:], rd[k * P : (k + 1) * P, NH:N])
+        wg_sb = [held.tile([P, CB, WCOLS], BF16, name=f"wg{w}") for w in range(WLOADS)]
+        wu_sb = [held.tile([P, CB, WCOLS], BF16, name=f"wu{w}") for w in range(WLOADS)]
+        for w in range(WLOADS):
+            cols = slice(w * WCOLS, (w + 1) * WCOLS)
+            nc.sync.dma_start(wg_sb[w][:], w_gate[:, cols].rearrange("(c p) i -> p c i", p=P))
+            nc.sync.dma_start(wu_sb[w][:], w_up[:, cols].rearrange("(c p) i -> p c i", p=P))
+        wd_sb = [held.tile([P, WB, D], BF16, name=f"wd{w}") for w in range(WLOADS)]
+        for w in range(WLOADS):
+            rows = slice(w * WCOLS, (w + 1) * WCOLS)
+            nc.sync.dma_start(wd_sb[w][:], w_down[rows, :].rearrange("(i p) c -> p i c", p=P))
+        hw_sb = held.tile([P, CB, V], BF16, name="hw")
+        nc.sync.dma_start(hw_sb[:], head_w.rearrange("(c p) m -> p c m", p=P))
+
+        ones = held.tile([P, P], BF16, name="ones")
+        nc.vector.memset(ones[:], 1.0)
+        eps = held.tile([P, 1], F32, name="eps")
+        nc.vector.memset(eps[:], EPS)
+
+        x0 = [[held.tile([P, NH], F32, name=f"x0_{h}_{c}") for c in range(CB)] for h in range(HALVES)]
+        x1 = [[held.tile([P, NH], F32, name=f"x1_{h}_{c}") for c in range(CB)] for h in range(HALVES)]
+        hn = [[held.tile([P, NH], BF16, name=f"hn_{h}_{c}") for c in range(CB)] for h in range(HALVES)]
+        yn = [[held.tile([P, NH], BF16, name=f"yn_{h}_{c}") for c in range(CB)] for h in range(HALVES)]
+        av = [[held.tile([P, NH], BF16, name=f"av_{h}_{i}") for i in range(IB)] for h in range(HALVES)]
+
+        def embed(h, order):
+            p_ps = [acc.tile([P, NH], F32, name=f"p_ps{c}", tag="acc") for c in range(CB)]
+            for k, c in order:
+                nc.tensor.matmul(
+                    p_ps[c][:], rw_sb[k][:, c * P : (c + 1) * P], rd_sb[h][k][:], start=(k == 0), stop=(k == VB - 1)
+                )
+            for c in range(CB):
+                p_sb = work.tile([P, NH], F32, name="p_sb")
+                nc.scalar.copy(p_sb[:], p_ps[c][:])
+                picked = emb_sb[c][:].indirect(offsets[:, h * (NH // 16) : (h + 1) * (NH // 16)])
+                nc.vector.tensor_tensor(x0[h][c][:], picked, p_sb[:], ALU.add)
+
+        def rms_norm(x, gain, dst):
+            ss_ps = stat.tile([P, NH], F32, name="ss_ps")
+            for c in range(CB):
+                sq = work.tile([P, NH], BF16, name="sq")
+                nc.scalar.activation(sq[:], x[c][:], ACT.Square)
+                nc.tensor.matmul(ss_ps[:], ones[:], sq[:], start=(c == 0), stop=(c == CB - 1))
+            rstd = work.tile([P, NH], F32, name="rstd")
+            nc.scalar.activation(rstd[:], ss_ps[:], ACT.Abs_reciprocal_sqrt, bias=eps[:], scale=1.0 / D)
+            for c in range(CB):
+                nc.vector.scalar_tensor_tensor(
+                    out=dst[c][:], in0=x[c][:], scalar=gain[:, c : c + 1], in1=rstd[:], op0=ALU.mult, op1=ALU.mult
+                )
+
+        def gated(h):
+            for i in range(IB):
+                cols = slice((i % WB) * P, (i % WB + 1) * P)
+                g_ps = acc.tile([P, NH], F32, name="g_ps", tag="acc")
+                u_ps = acc.tile([P, NH], F32, name="u_ps", tag="acc")
+                for c in range(CB):
+                    nc.tensor.matmul(g_ps[:], wg_sb[i // WB][:, c, cols], hn[h][c][:], start=(c == 0), stop=(c == CB - 1))
+                for c in range(CB):
+                    nc.tensor.matmul(u_ps[:], wu_sb[i // WB][:, c, cols], hn[h][c][:], start=(c == 0), stop=(c == CB - 1))
+                sil = work.tile([P, NH], F32, name="sil")
+                nc.scalar.activation(sil[:], g_ps[:], ACT.Silu)
+                nc.vector.tensor_tensor(av[h][i][:], sil[:], u_ps[:], ALU.mult)
+
+        def down(h):
+            for c in range(CB):
+                d_ps = acc.tile([P, NH], F32, name="d_ps", tag="acc")
+                for i in range(IB):
+                    nc.tensor.matmul(
+                        d_ps[:], wd_sb[i // WB][:, i % WB, c * P : (c + 1) * P], av[h][i][:], start=(i == 0), stop=(i == IB - 1)
+                    )
+                nc.vector.tensor_tensor(x1[h][c][:], x0[h][c][:], d_ps[:], ALU.add)
+
+        def head(h):
+            for m in range(VB):
+                l_ps = acc.tile([P, NH], F32, name="l_ps", tag="acc")
+                for c in range(CB):
+                    nc.tensor.matmul(l_ps[:], hw_sb[:, c, m * P : (m + 1) * P], yn[h][c][:], start=(c == 0), stop=(c == CB - 1))
+                l_sb = work.tile([P, NH], F32, name="l_sb")
+                if m % 2 == 0:
+                    nc.scalar.copy(l_sb[:], l_ps[:])
+                else:
+                    nc.vector.tensor_copy(l_sb[:], l_ps[:])
+                nc.sync.dma_start(out[m * P : (m + 1) * P, h * NH : (h + 1) * NH], l_sb[:])
+
+        embed(0, [(k, c) for k in range(VB) for c in range(CB)])
+        rms_norm(x0[0], gain1, hn[0])
+        embed(1, [(k, c) for c in range(CB) for k in range(VB)])
+        rms_norm(x0[1], gain1, hn[1])
+        gated(0)
+        gated(1)
+        down(0)
+        rms_norm(x1[0], gain2, yn[0])
+        down(1)
+        rms_norm(x1[1], gain2, yn[1])
+        head(0)
+        head(1)

@@ -15,6 +15,7 @@ VB, CB, IB = V // P, D // P, HID // P
 WCOLS = 512
 WB = WCOLS // P
 WLOADS = HID // WCOLS
+WARM = 3
 
 FLOPS = 2 * N * (V * D + 2 * D * HID + HID * D + D * V)
 
@@ -43,8 +44,11 @@ def tile_residualbitnettransformer_b_kernel(
         nc.scalar.dma_start(gain2[:], norm_gain.rearrange("(a p) o -> p (a o)", p=P))
         for c in range(CB):
             nc.sync.dma_start(emb_sb[c][:], emb[c * P : (c + 1) * P, :])
-            for k in (2 * c, 2 * c + 1):
-                nc.sync.dma_start(rd_sb[1][k][:], rd[k * P : (k + 1) * P, NH:N])
+            if c % 2 == 1:
+                for k in (c - 1, c):
+                    nc.sync.dma_start(rd_sb[1][k][:], rd[k * P : (k + 1) * P, NH:N])
+        for k in range(VB // 2, VB):
+            nc.sync.dma_start(rd_sb[1][k][:], rd[k * P : (k + 1) * P, NH:N])
         wg_sb = [held.tile([P, CB, WCOLS], BF16, name=f"wg{w}") for w in range(WLOADS)]
         wu_sb = [held.tile([P, CB, WCOLS], BF16, name=f"wu{w}") for w in range(WLOADS)]
         for w in range(WLOADS):
@@ -58,8 +62,9 @@ def tile_residualbitnettransformer_b_kernel(
         hw_sb = held.tile([P, CB, V], BF16, name="hw")
         nc.sync.dma_start(hw_sb[:], head_w.rearrange("(c p) m -> p c m", p=P))
 
-        ones = held.tile([P, P], BF16, name="ones")
+        ones = held.tile([P, NH], BF16, name="ones")
         nc.vector.memset(ones[:], 1.0)
+        sum_w = ones[:, 0:P]
         eps = held.tile([P, 1], F32, name="eps")
         nc.vector.memset(eps[:], EPS)
 
@@ -69,24 +74,43 @@ def tile_residualbitnettransformer_b_kernel(
         yn = [[held.tile([P, NH], BF16, name=f"yn_{h}_{c}") for c in range(CB)] for h in range(HALVES)]
         av = [[held.tile([P, NH], BF16, name=f"av_{h}_{i}") for i in range(IB)] for h in range(HALVES)]
 
-        def embed(h, order):
-            p_ps = [acc.tile([P, NH], F32, name=f"p_ps{c}", tag="acc") for c in range(CB)]
-            for k, c in order:
-                nc.tensor.matmul(
-                    p_ps[c][:], rw_sb[k][:, c * P : (c + 1) * P], rd_sb[h][k][:], start=(k == 0), stop=(k == VB - 1)
-                )
-            for c in range(CB):
-                p_sb = work.tile([P, NH], F32, name="p_sb")
-                nc.scalar.copy(p_sb[:], p_ps[c][:])
-                picked = emb_sb[c][:].indirect(offsets[:, h * (NH // 16) : (h + 1) * (NH // 16)])
-                nc.vector.tensor_tensor(x0[h][c][:], picked, p_sb[:], ALU.add)
+        def project(p_ps, h, k, c):
+            nc.tensor.matmul(
+                p_ps[:], rw_sb[k][:, c * P : (c + 1) * P], rd_sb[h][k][:], start=(k == 0), stop=(k == VB - 1)
+            )
 
-        def rms_norm(x, gain, dst):
-            ss_ps = stat.tile([P, NH], F32, name="ss_ps")
+        def embed_begin(h):
+            p_ps = [acc.tile([P, NH], F32, name=f"p_ps{c}", tag="acc") for c in range(CB)]
+            for k in range(VB // 2):
+                for c in range(CB):
+                    project(p_ps[c], h, k, c)
+            return p_ps
+
+        def embed_end(h, p_ps):
+            for c in range(CB):
+                for k in range(VB // 2, VB):
+                    project(p_ps[c], h, k, c)
+                look_up(p_ps[c], h, c)
+
+        def look_up(p_ps, h, c):
+            p_sb = work.tile([P, NH], F32, name="p_sb")
+            nc.scalar.copy(p_sb[:], p_ps[:])
+            picked = emb_sb[c][:].indirect(offsets[:, h * (NH // 16) : (h + 1) * (NH // 16)])
+            nc.vector.tensor_tensor(x0[h][c][:], picked, p_sb[:], ALU.add)
+
+        def sum_squares(x):
+            total = None
             for c in range(CB):
                 sq = work.tile([P, NH], BF16, name="sq")
                 nc.scalar.activation(sq[:], x[c][:], ACT.Square)
-                nc.tensor.matmul(ss_ps[:], ones[:], sq[:], start=(c == 0), stop=(c == CB - 1))
+                if c > 0:
+                    nc.vector.tensor_tensor(sq[:], sq[:], total[:], ALU.add)
+                total = sq
+            return total
+
+        def rms_norm(x, total, gain, dst):
+            ss_ps = stat.tile([P, NH], F32, name="ss_ps")
+            nc.tensor.matmul(ss_ps[:], sum_w, total[:], start=True, stop=True)
             rstd = work.tile([P, NH], F32, name="rstd")
             nc.scalar.activation(rstd[:], ss_ps[:], ACT.Abs_reciprocal_sqrt, bias=eps[:], scale=1.0 / D)
             for c in range(CB):
@@ -94,49 +118,65 @@ def tile_residualbitnettransformer_b_kernel(
                     out=dst[c][:], in0=x[c][:], scalar=gain[:, c : c + 1], in1=rstd[:], op0=ALU.mult, op1=ALU.mult
                 )
 
-        def gated(h):
-            for i in range(IB):
-                cols = slice((i % WB) * P, (i % WB + 1) * P)
-                g_ps = acc.tile([P, NH], F32, name="g_ps", tag="acc")
-                u_ps = acc.tile([P, NH], F32, name="u_ps", tag="acc")
-                for c in range(CB):
-                    nc.tensor.matmul(g_ps[:], wg_sb[i // WB][:, c, cols], hn[h][c][:], start=(c == 0), stop=(c == CB - 1))
-                for c in range(CB):
-                    nc.tensor.matmul(u_ps[:], wu_sb[i // WB][:, c, cols], hn[h][c][:], start=(c == 0), stop=(c == CB - 1))
-                sil = work.tile([P, NH], F32, name="sil")
-                nc.scalar.activation(sil[:], g_ps[:], ACT.Silu)
-                nc.vector.tensor_tensor(av[h][i][:], sil[:], u_ps[:], ALU.mult)
-
-        def down(h):
+        def gated(h, i):
+            cols = slice((i % WB) * P, (i % WB + 1) * P)
+            g_ps = acc.tile([P, NH], F32, name="g_ps", tag="acc")
+            u_ps = acc.tile([P, NH], F32, name="u_ps", tag="acc")
             for c in range(CB):
-                d_ps = acc.tile([P, NH], F32, name="d_ps", tag="acc")
-                for i in range(IB):
-                    nc.tensor.matmul(
-                        d_ps[:], wd_sb[i // WB][:, i % WB, c * P : (c + 1) * P], av[h][i][:], start=(i == 0), stop=(i == IB - 1)
-                    )
-                nc.vector.tensor_tensor(x1[h][c][:], x0[h][c][:], d_ps[:], ALU.add)
+                nc.tensor.matmul(g_ps[:], wg_sb[i // WB][:, c, cols], hn[h][c][:], start=(c == 0), stop=(c == CB - 1))
+            for c in range(CB):
+                nc.tensor.matmul(u_ps[:], wu_sb[i // WB][:, c, cols], hn[h][c][:], start=(c == 0), stop=(c == CB - 1))
+            sil = work.tile([P, NH], F32, name="sil")
+            nc.scalar.activation(sil[:], g_ps[:], ACT.Silu)
+            nc.vector.tensor_tensor(av[h][i][:], sil[:], u_ps[:], ALU.mult)
 
-        def head(h):
-            for m in range(VB):
-                l_ps = acc.tile([P, NH], F32, name="l_ps", tag="acc")
-                for c in range(CB):
-                    nc.tensor.matmul(l_ps[:], hw_sb[:, c, m * P : (m + 1) * P], yn[h][c][:], start=(c == 0), stop=(c == CB - 1))
-                l_sb = work.tile([P, NH], F32, name="l_sb")
-                if m % 2 == 0:
-                    nc.scalar.copy(l_sb[:], l_ps[:])
-                else:
-                    nc.vector.tensor_copy(l_sb[:], l_ps[:])
-                nc.sync.dma_start(out[m * P : (m + 1) * P, h * NH : (h + 1) * NH], l_sb[:])
+        def down(h, c):
+            d_ps = acc.tile([P, NH], F32, name="d_ps", tag="acc")
+            for i in range(IB):
+                nc.tensor.matmul(
+                    d_ps[:], wd_sb[i // WB][:, i % WB, c * P : (c + 1) * P], av[h][i][:], start=(i == 0), stop=(i == IB - 1)
+                )
+            nc.vector.tensor_tensor(x1[h][c][:], x0[h][c][:], d_ps[:], ALU.add)
 
-        embed(0, [(k, c) for k in range(VB) for c in range(CB)])
-        rms_norm(x0[0], gain1, hn[0])
-        embed(1, [(k, c) for c in range(CB) for k in range(VB)])
-        rms_norm(x0[1], gain1, hn[1])
-        gated(0)
-        gated(1)
-        down(0)
-        rms_norm(x1[0], gain2, yn[0])
-        down(1)
-        rms_norm(x1[1], gain2, yn[1])
-        head(0)
-        head(1)
+        def head(h, m):
+            l_ps = acc.tile([P, NH], F32, name="l_ps", tag="acc")
+            for c in range(CB):
+                nc.tensor.matmul(l_ps[:], hw_sb[:, c, m * P : (m + 1) * P], yn[h][c][:], start=(c == 0), stop=(c == CB - 1))
+            l_sb = work.tile([P, NH], F32, name="l_sb")
+            if m % 2 == 0:
+                nc.scalar.copy(l_sb[:], l_ps[:])
+            else:
+                nc.vector.tensor_copy(l_sb[:], l_ps[:])
+            nc.sync.dma_start(out[m * P : (m + 1) * P, h * NH : (h + 1) * NH], l_sb[:])
+
+
+        warm_ps = stat.tile([P, NH], F32, name="warm_ps", tag="ss_ps")
+        for r in range(WARM):
+            nc.tensor.matmul(warm_ps[:], sum_w, ones[:], start=True, stop=True)
+
+        embed_end(0, embed_begin(0))
+        total = sum_squares(x0[0])
+        p_ps = embed_begin(1)
+        rms_norm(x0[0], total, gain1, hn[0])
+        embed_end(1, p_ps)
+        for i in range(IB):
+            gated(0, i)
+        total = sum_squares(x0[1])
+        for c in range(CB):
+            down(0, c)
+            if c == 0:
+                rms_norm(x0[1], total, gain1, hn[1])
+        for i in range(IB):
+            gated(1, i)
+        total = sum_squares(x1[0])
+        for c in range(CB):
+            down(1, c)
+            if c == 0:
+                rms_norm(x1[0], total, gain2, yn[0])
+        total = sum_squares(x1[1])
+        for m in range(VB):
+            head(0, m)
+            if m == 2:
+                rms_norm(x1[1], total, gain2, yn[1])
+        for m in range(VB):
+            head(1, m)

@@ -15,7 +15,6 @@ VB, CB, IB = V // P, D // P, HID // P
 WCOLS = 512
 WB = WCOLS // P
 WLOADS = HID // WCOLS
-WARM = 3
 
 FLOPS = 2 * N * (V * D + 2 * D * HID + HID * D + D * V)
 
@@ -62,9 +61,8 @@ def tile_residualbitnettransformer_b_kernel(
         hw_sb = held.tile([P, CB, V], BF16, name="hw")
         nc.sync.dma_start(hw_sb[:], head_w.rearrange("(c p) m -> p c m", p=P))
 
-        ones = held.tile([P, NH], BF16, name="ones")
+        ones = held.tile([P, P], BF16, name="ones")
         nc.vector.memset(ones[:], 1.0)
-        sum_w = ones[:, 0:P]
         eps = held.tile([P, 1], F32, name="eps")
         nc.vector.memset(eps[:], EPS)
 
@@ -110,7 +108,7 @@ def tile_residualbitnettransformer_b_kernel(
 
         def rms_norm(x, total, gain, dst):
             ss_ps = stat.tile([P, NH], F32, name="ss_ps")
-            nc.tensor.matmul(ss_ps[:], sum_w, total[:], start=True, stop=True)
+            nc.tensor.matmul(ss_ps[:], ones[:], total[:], start=True, stop=True)
             rstd = work.tile([P, NH], F32, name="rstd")
             nc.scalar.activation(rstd[:], ss_ps[:], ACT.Abs_reciprocal_sqrt, bias=eps[:], scale=1.0 / D)
             for c in range(CB):
@@ -149,10 +147,6 @@ def tile_residualbitnettransformer_b_kernel(
                 nc.vector.tensor_copy(l_sb[:], l_ps[:])
             nc.sync.dma_start(out[m * P : (m + 1) * P, h * NH : (h + 1) * NH], l_sb[:])
 
-
-        warm_ps = stat.tile([P, NH], F32, name="warm_ps", tag="ss_ps")
-        for r in range(WARM):
-            nc.tensor.matmul(warm_ps[:], sum_w, ones[:], start=True, stop=True)
 
         embed_end(0, embed_begin(0))
         total = sum_squares(x0[0])

@@ -15,6 +15,8 @@ VB, CB, IB = V // P, D // P, HID // P
 WCOLS = 512
 WB = WCOLS // P
 WLOADS = HID // WCOLS
+GROWING = (0, 1, 2, 4, 8)
+LEAD = 12
 
 FLOPS = 2 * N * (V * D + 2 * D * HID + HID * D + D * V)
 
@@ -29,12 +31,18 @@ def tile_residualbitnettransformer_b_kernel(
         tc.psum_pool(name="acc", bufs=6) as acc,
         tc.psum_pool(name="stat", bufs=2) as stat,
     ):
-        rd_sb = [[held.tile([P, NH], BF16, name=f"rd{h}_{k}") for k in range(VB)] for h in range(HALVES)]
-        rw_sb = [held.tile([P, D], BF16, name=f"rw{k}") for k in range(VB)]
+        rd_sb = [held.tile([P, VB, NH], BF16, name=f"rd{half}") for half in range(HALVES)]
+        rw_sb = held.tile([P, VB, D], BF16, name="rw")
+
+        def load_rd(half, first, last):
+            rows = rd[first * P : last * P, half * NH : (half + 1) * NH]
+            nc.sync.dma_start(rd_sb[half][:, first:last, :], rows.rearrange("(k p) j -> p k j", p=P))
+
         emb_sb = [held.tile([P, V], F32, name=f"emb{c}") for c in range(CB)]
-        for k in range(VB):
-            nc.sync.dma_start(rd_sb[0][k][:], rd[k * P : (k + 1) * P, 0:NH])
-            nc.scalar.dma_start(rw_sb[k][:], resid_w[k * P : (k + 1) * P, :])
+        for first, last in zip(GROWING, GROWING[1:]):
+            load_rd(0, first, last)
+            rows = resid_w[first * P : last * P, :]
+            nc.scalar.dma_start(rw_sb[:, first:last, :], rows.rearrange("(k p) c -> p k c", p=P))
         offsets = held.tile([P, N // 16], U16, name="offsets")
         nc.sync.dma_start(offsets[:], offs)
         gain1 = held.tile([P, CB], F32, name="gain1")
@@ -44,20 +52,18 @@ def tile_residualbitnettransformer_b_kernel(
         for c in range(CB):
             nc.sync.dma_start(emb_sb[c][:], emb[c * P : (c + 1) * P, :])
             if c % 2 == 1:
-                for k in (c - 1, c):
-                    nc.sync.dma_start(rd_sb[1][k][:], rd[k * P : (k + 1) * P, NH:N])
-        for k in range(VB // 2, VB):
-            nc.sync.dma_start(rd_sb[1][k][:], rd[k * P : (k + 1) * P, NH:N])
+                load_rd(1, c - 1, c + 1)
+        load_rd(1, VB // 2, VB)
         wg_sb = [held.tile([P, CB, WCOLS], BF16, name=f"wg{w}") for w in range(WLOADS)]
         wu_sb = [held.tile([P, CB, WCOLS], BF16, name=f"wu{w}") for w in range(WLOADS)]
         for w in range(WLOADS):
-            cols = slice(w * WCOLS, (w + 1) * WCOLS)
-            nc.sync.dma_start(wg_sb[w][:], w_gate[:, cols].rearrange("(c p) i -> p c i", p=P))
-            nc.sync.dma_start(wu_sb[w][:], w_up[:, cols].rearrange("(c p) i -> p c i", p=P))
+            units = slice(w * WCOLS, (w + 1) * WCOLS)
+            nc.sync.dma_start(wg_sb[w][:], w_gate[:, units].rearrange("(c p) i -> p c i", p=P))
+            nc.sync.dma_start(wu_sb[w][:], w_up[:, units].rearrange("(c p) i -> p c i", p=P))
         wd_sb = [held.tile([P, WB, D], BF16, name=f"wd{w}") for w in range(WLOADS)]
         for w in range(WLOADS):
-            rows = slice(w * WCOLS, (w + 1) * WCOLS)
-            nc.sync.dma_start(wd_sb[w][:], w_down[rows, :].rearrange("(i p) c -> p i c", p=P))
+            units = slice(w * WCOLS, (w + 1) * WCOLS)
+            nc.sync.dma_start(wd_sb[w][:], w_down[units, :].rearrange("(i p) c -> p i c", p=P))
         hw_sb = held.tile([P, CB, V], BF16, name="hw")
         nc.sync.dma_start(hw_sb[:], head_w.rearrange("(c p) m -> p c m", p=P))
 
@@ -66,35 +72,35 @@ def tile_residualbitnettransformer_b_kernel(
         eps = held.tile([P, 1], F32, name="eps")
         nc.vector.memset(eps[:], EPS)
 
-        x0 = [[held.tile([P, NH], F32, name=f"x0_{h}_{c}") for c in range(CB)] for h in range(HALVES)]
-        x1 = [[held.tile([P, NH], F32, name=f"x1_{h}_{c}") for c in range(CB)] for h in range(HALVES)]
-        hn = [[held.tile([P, NH], BF16, name=f"hn_{h}_{c}") for c in range(CB)] for h in range(HALVES)]
-        yn = [[held.tile([P, NH], BF16, name=f"yn_{h}_{c}") for c in range(CB)] for h in range(HALVES)]
-        av = [[held.tile([P, NH], BF16, name=f"av_{h}_{i}") for i in range(IB)] for h in range(HALVES)]
+        x0 = [[held.tile([P, NH], F32, name=f"x0_{half}_{c}") for c in range(CB)] for half in range(HALVES)]
+        x1 = [[held.tile([P, NH], F32, name=f"x1_{half}_{c}") for c in range(CB)] for half in range(HALVES)]
+        hn = [[held.tile([P, NH], BF16, name=f"hn_{half}_{c}") for c in range(CB)] for half in range(HALVES)]
+        yn = [[held.tile([P, NH], BF16, name=f"yn_{half}_{c}") for c in range(CB)] for half in range(HALVES)]
+        av = [[held.tile([P, NH], BF16, name=f"av_{half}_{i}") for i in range(IB)] for half in range(HALVES)]
 
-        def project(p_ps, h, k, c):
+        def project(bank, half, k, c):
             nc.tensor.matmul(
-                p_ps[:], rw_sb[k][:, c * P : (c + 1) * P], rd_sb[h][k][:], start=(k == 0), stop=(k == VB - 1)
+                bank[:], rw_sb[:, k, c * P : (c + 1) * P], rd_sb[half][:, k, :], start=(k == 0), stop=(k == VB - 1)
             )
 
-        def embed_begin(h):
-            p_ps = [acc.tile([P, NH], F32, name=f"p_ps{c}", tag="acc") for c in range(CB)]
+        def embed_begin(half):
+            banks = [acc.tile([P, NH], F32, name=f"p_ps{c}", tag="acc") for c in range(CB)]
             for k in range(VB // 2):
                 for c in range(CB):
-                    project(p_ps[c], h, k, c)
-            return p_ps
+                    project(banks[c], half, k, c)
+            return banks
 
-        def embed_end(h, p_ps):
+        def embed_end(half, banks):
             for c in range(CB):
                 for k in range(VB // 2, VB):
-                    project(p_ps[c], h, k, c)
-                look_up(p_ps[c], h, c)
+                    project(banks[c], half, k, c)
+                look_up(banks[c], half, c)
 
-        def look_up(p_ps, h, c):
+        def look_up(bank, half, c):
             p_sb = work.tile([P, NH], F32, name="p_sb")
-            nc.scalar.copy(p_sb[:], p_ps[:])
-            picked = emb_sb[c][:].indirect(offsets[:, h * (NH // 16) : (h + 1) * (NH // 16)])
-            nc.vector.tensor_tensor(x0[h][c][:], picked, p_sb[:], ALU.add)
+            nc.scalar.copy(p_sb[:], bank[:])
+            picked = emb_sb[c][:].indirect(offsets[:, half * (NH // 16) : (half + 1) * (NH // 16)])
+            nc.vector.tensor_tensor(x0[half][c][:], picked, p_sb[:], ALU.add)
 
         def sum_squares(x):
             total = None
@@ -116,61 +122,60 @@ def tile_residualbitnettransformer_b_kernel(
                     out=dst[c][:], in0=x[c][:], scalar=gain[:, c : c + 1], in1=rstd[:], op0=ALU.mult, op1=ALU.mult
                 )
 
-        def gated(h, i):
+        def gated(half, i):
             cols = slice((i % WB) * P, (i % WB + 1) * P)
             g_ps = acc.tile([P, NH], F32, name="g_ps", tag="acc")
             u_ps = acc.tile([P, NH], F32, name="u_ps", tag="acc")
             for c in range(CB):
-                nc.tensor.matmul(g_ps[:], wg_sb[i // WB][:, c, cols], hn[h][c][:], start=(c == 0), stop=(c == CB - 1))
+                nc.tensor.matmul(g_ps[:], wg_sb[i // WB][:, c, cols], hn[half][c][:], start=(c == 0), stop=(c == CB - 1))
             for c in range(CB):
-                nc.tensor.matmul(u_ps[:], wu_sb[i // WB][:, c, cols], hn[h][c][:], start=(c == 0), stop=(c == CB - 1))
+                nc.tensor.matmul(u_ps[:], wu_sb[i // WB][:, c, cols], hn[half][c][:], start=(c == 0), stop=(c == CB - 1))
             sil = work.tile([P, NH], F32, name="sil")
             nc.scalar.activation(sil[:], g_ps[:], ACT.Silu)
-            nc.vector.tensor_tensor(av[h][i][:], sil[:], u_ps[:], ALU.mult)
+            nc.vector.tensor_tensor(av[half][i][:], sil[:], u_ps[:], ALU.mult)
 
-        def down(h, c):
+        def down(half, c):
             d_ps = acc.tile([P, NH], F32, name="d_ps", tag="acc")
             for i in range(IB):
                 nc.tensor.matmul(
-                    d_ps[:], wd_sb[i // WB][:, i % WB, c * P : (c + 1) * P], av[h][i][:], start=(i == 0), stop=(i == IB - 1)
+                    d_ps[:], wd_sb[i // WB][:, i % WB, c * P : (c + 1) * P], av[half][i][:], start=(i == 0), stop=(i == IB - 1)
                 )
-            nc.vector.tensor_tensor(x1[h][c][:], x0[h][c][:], d_ps[:], ALU.add)
+            nc.vector.tensor_tensor(x1[half][c][:], x0[half][c][:], d_ps[:], ALU.add)
 
-        def head(h, m):
+        def head(half, m):
             l_ps = acc.tile([P, NH], F32, name="l_ps", tag="acc")
             for c in range(CB):
-                nc.tensor.matmul(l_ps[:], hw_sb[:, c, m * P : (m + 1) * P], yn[h][c][:], start=(c == 0), stop=(c == CB - 1))
+                nc.tensor.matmul(l_ps[:], hw_sb[:, c, m * P : (m + 1) * P], yn[half][c][:], start=(c == 0), stop=(c == CB - 1))
             l_sb = work.tile([P, NH], F32, name="l_sb")
             if m % 2 == 0:
                 nc.scalar.copy(l_sb[:], l_ps[:])
             else:
                 nc.vector.tensor_copy(l_sb[:], l_ps[:])
-            nc.sync.dma_start(out[m * P : (m + 1) * P, h * NH : (h + 1) * NH], l_sb[:])
-
+            nc.sync.dma_start(out[m * P : (m + 1) * P, half * NH : (half + 1) * NH], l_sb[:])
 
         embed_end(0, embed_begin(0))
         total = sum_squares(x0[0])
-        p_ps = embed_begin(1)
+        banks = embed_begin(1)
         rms_norm(x0[0], total, gain1, hn[0])
-        embed_end(1, p_ps)
+        embed_end(1, banks)
         for i in range(IB):
             gated(0, i)
         total = sum_squares(x0[1])
         for c in range(CB):
             down(0, c)
-            if c == 0:
+            if (c + 1) * IB == LEAD:
                 rms_norm(x0[1], total, gain1, hn[1])
         for i in range(IB):
             gated(1, i)
         total = sum_squares(x1[0])
         for c in range(CB):
             down(1, c)
-            if c == 0:
+            if (c + 1) * IB == LEAD:
                 rms_norm(x1[0], total, gain2, yn[0])
         total = sum_squares(x1[1])
         for m in range(VB):
             head(0, m)
-            if m == 2:
+            if (m + 1) * CB == LEAD:
                 rms_norm(x1[1], total, gain2, yn[1])
         for m in range(VB):
             head(1, m)

@@ -16,6 +16,7 @@ WCOLS = 512
 WB = WCOLS // P
 WLOADS = HID // WCOLS
 GROWING = (0, 1, 2, 4, 8)
+WARM = 3
 LEAD = 12
 
 FLOPS = 2 * N * (V * D + 2 * D * HID + HID * D + D * V)
@@ -67,8 +68,9 @@ def tile_residualbitnettransformer_b_kernel(
         hw_sb = held.tile([P, CB, V], BF16, name="hw")
         nc.sync.dma_start(hw_sb[:], head_w.rearrange("(c p) m -> p c m", p=P))
 
-        ones = held.tile([P, P], BF16, name="ones")
+        ones = held.tile([P, NH], BF16, name="ones")
         nc.vector.memset(ones[:], 1.0)
+        sum_w = ones[:, 0:P]
         eps = held.tile([P, 1], F32, name="eps")
         nc.vector.memset(eps[:], EPS)
 
@@ -114,7 +116,7 @@ def tile_residualbitnettransformer_b_kernel(
 
         def rms_norm(x, total, gain, dst):
             ss_ps = stat.tile([P, NH], F32, name="ss_ps")
-            nc.tensor.matmul(ss_ps[:], ones[:], total[:], start=True, stop=True)
+            nc.tensor.matmul(ss_ps[:], sum_w, total[:], start=True, stop=True)
             rstd = work.tile([P, NH], F32, name="rstd")
             nc.scalar.activation(rstd[:], ss_ps[:], ACT.Abs_reciprocal_sqrt, bias=eps[:], scale=1.0 / D)
             for c in range(CB):
@@ -153,6 +155,9 @@ def tile_residualbitnettransformer_b_kernel(
                 nc.vector.tensor_copy(l_sb[:], l_ps[:])
             nc.sync.dma_start(out[m * P : (m + 1) * P, half * NH : (half + 1) * NH], l_sb[:])
 
+        warm_ps = stat.tile([P, NH], F32, name="warm_ps", tag="ss_ps")
+        for r in range(WARM):
+            nc.tensor.matmul(warm_ps[:], sum_w, ones[:], start=True, stop=True)
         embed_end(0, embed_begin(0))
         total = sum_squares(x0[0])
         banks = embed_begin(1)

@@ -16,7 +16,6 @@ WCOLS = 512
 WB = WCOLS // P
 WLOADS = HID // WCOLS
 GROWING = (0, 1, 2, 4, 8)
-WARM = 3
 LEAD = 12
 
 FLOPS = 2 * N * (V * D + 2 * D * HID + HID * D + D * V)
@@ -68,9 +67,9 @@ def tile_residualbitnettransformer_b_kernel(
         hw_sb = held.tile([P, CB, V], BF16, name="hw")
         nc.sync.dma_start(hw_sb[:], head_w.rearrange("(c p) m -> p c m", p=P))
 
-        ones = held.tile([P, NH], BF16, name="ones")
+        ones = held.tile([P, P], BF16, name="ones")
         nc.vector.memset(ones[:], 1.0)
-        sum_w = ones[:, 0:P]
+        sum_w = ones[:]
         eps = held.tile([P, 1], F32, name="eps")
         nc.vector.memset(eps[:], EPS)
 
@@ -155,9 +154,6 @@ def tile_residualbitnettransformer_b_kernel(
                 nc.vector.tensor_copy(l_sb[:], l_ps[:])
             nc.sync.dma_start(out[m * P : (m + 1) * P, half * NH : (half + 1) * NH], l_sb[:])
 
-        warm_ps = stat.tile([P, NH], F32, name="warm_ps", tag="ss_ps")
-        for r in range(WARM):
-            nc.tensor.matmul(warm_ps[:], sum_w, ones[:], start=True, stop=True)
         embed_end(0, embed_begin(0))
         total = sum_squares(x0[0])
         banks = embed_begin(1)

@@ -16,6 +16,7 @@ WCOLS = 512
 WB = WCOLS // P
 WLOADS = HID // WCOLS
 GROWING = (0, 1, 2, 4, 8)
+WARM = 12
 LEAD = 12
 
 FLOPS = 2 * N * (V * D + 2 * D * HID + HID * D + D * V)
@@ -68,7 +69,7 @@ def tile_residualbitnettransformer_b_kernel(
         nc.sync.dma_start(hw_sb[:], head_w.rearrange("(c p) m -> p c m", p=P))
 
         ones = held.tile([P, P], BF16, name="ones")
-        nc.vector.memset(ones[:], 1.0)
+        nc.gpsimd.memset(ones[:], 1.0)
         sum_w = ones[:]
         eps = held.tile([P, 1], F32, name="eps")
         nc.vector.memset(eps[:], EPS)
@@ -154,6 +155,9 @@ def tile_residualbitnettransformer_b_kernel(
                 nc.vector.tensor_copy(l_sb[:], l_ps[:])
             nc.sync.dma_start(out[m * P : (m + 1) * P, half * NH : (half + 1) * NH], l_sb[:])
 
+        warm_ps = stat.tile([P, P], F32, name="warm_ps", tag="ss_ps")
+        for r in range(WARM):
+            nc.tensor.matmul(warm_ps[:], sum_w, ones[:], start=True, stop=True)
         embed_end(0, embed_begin(0))
         total = sum_squares(x0[0])
         banks = embed_begin(1)

@@ -16,6 +16,8 @@ WCOLS = 512
 WB = WCOLS // P
 WLOADS = HID // WCOLS
 GROWING = (0, 1, 2, 4, 8)
+CUT = (4, 5)
+PAIR = 2
 WARM = 12
 LEAD = 12
 
@@ -29,8 +31,7 @@ def tile_residualbitnettransformer_b_kernel(
     with (
         tc.tile_pool(name="held", bufs=1) as held,
         tc.tile_pool(name="work", bufs=4) as work,
-        tc.psum_pool(name="acc", bufs=6) as acc,
-        tc.psum_pool(name="stat", bufs=2) as stat,
+        tc.psum_pool(name="acc", bufs=8) as acc,
     ):
         rd_sb = [held.tile([P, VB, NH], BF16, name=f"rd{half}") for half in range(HALVES)]
         rw_sb = held.tile([P, VB, D], BF16, name="rw")
@@ -87,14 +88,14 @@ def tile_residualbitnettransformer_b_kernel(
 
         def embed_begin(half):
             banks = [acc.tile([P, NH], F32, name=f"p_ps{c}", tag="acc") for c in range(CB)]
-            for k in range(VB // 2):
+            for k in range(CUT[half]):
                 for c in range(CB):
                     project(banks[c], half, k, c)
             return banks
 
         def embed_end(half, banks):
             for c in range(CB):
-                for k in range(VB // 2, VB):
+                for k in range(CUT[half], VB):
                     project(banks[c], half, k, c)
                 look_up(banks[c], half, c)
 
@@ -115,7 +116,7 @@ def tile_residualbitnettransformer_b_kernel(
             return total
 
         def rms_norm(x, total, gain, dst):
-            ss_ps = stat.tile([P, NH], F32, name="ss_ps")
+            ss_ps = acc.tile([P, NH], F32, name="ss_ps", tag="acc")
             nc.tensor.matmul(ss_ps[:], sum_w, total[:], start=True, stop=True)
             rstd = work.tile([P, NH], F32, name="rstd")
             nc.scalar.activation(rstd[:], ss_ps[:], ACT.Abs_reciprocal_sqrt, bias=eps[:], scale=1.0 / D)
@@ -124,17 +125,20 @@ def tile_residualbitnettransformer_b_kernel(
                     out=dst[c][:], in0=x[c][:], scalar=gain[:, c : c + 1], in1=rstd[:], op0=ALU.mult, op1=ALU.mult
                 )
 
-        def gated(half, i):
-            cols = slice((i % WB) * P, (i % WB + 1) * P)
-            g_ps = acc.tile([P, NH], F32, name="g_ps", tag="acc")
-            u_ps = acc.tile([P, NH], F32, name="u_ps", tag="acc")
+        def gated(half, blocks):
+            g_ps = {i: acc.tile([P, NH], F32, name="g_ps", tag="acc") for i in blocks}
+            u_ps = {i: acc.tile([P, NH], F32, name="u_ps", tag="acc") for i in blocks}
             for c in range(CB):
-                nc.tensor.matmul(g_ps[:], wg_sb[i // WB][:, c, cols], hn[half][c][:], start=(c == 0), stop=(c == CB - 1))
-            for c in range(CB):
-                nc.tensor.matmul(u_ps[:], wu_sb[i // WB][:, c, cols], hn[half][c][:], start=(c == 0), stop=(c == CB - 1))
-            sil = work.tile([P, NH], F32, name="sil")
-            nc.scalar.activation(sil[:], g_ps[:], ACT.Silu)
-            nc.vector.tensor_tensor(av[half][i][:], sil[:], u_ps[:], ALU.mult)
+                for banks, w_sb in ((g_ps, wg_sb), (u_ps, wu_sb)):
+                    for i in blocks:
+                        cols = slice((i % WB) * P, (i % WB + 1) * P)
+                        nc.tensor.matmul(
+                            banks[i][:], w_sb[i // WB][:, c, cols], hn[half][c][:], start=(c == 0), stop=(c == CB - 1)
+                        )
+            for i in blocks:
+                sil = work.tile([P, NH], F32, name="sil")
+                nc.scalar.activation(sil[:], g_ps[i][:], ACT.Silu)
+                nc.vector.tensor_tensor(av[half][i][:], sil[:], u_ps[i][:], ALU.mult)
 
         def down(half, c):
             d_ps = acc.tile([P, NH], F32, name="d_ps", tag="acc")
@@ -155,7 +159,7 @@ def tile_residualbitnettransformer_b_kernel(
                 nc.vector.tensor_copy(l_sb[:], l_ps[:])
             nc.sync.dma_start(out[m * P : (m + 1) * P, half * NH : (half + 1) * NH], l_sb[:])
 
-        warm_ps = stat.tile([P, P], F32, name="warm_ps", tag="ss_ps")
+        warm_ps = acc.tile([P, P], F32, name="warm_ps", tag="acc")
         for r in range(WARM):
             nc.tensor.matmul(warm_ps[:], sum_w, ones[:], start=True, stop=True)
         embed_end(0, embed_begin(0))
@@ -163,15 +167,15 @@ def tile_residualbitnettransformer_b_kernel(
         banks = embed_begin(1)
         rms_norm(x0[0], total, gain1, hn[0])
         embed_end(1, banks)
-        for i in range(IB):
-            gated(0, i)
+        for i in range(0, IB, PAIR):
+            gated(0, range(i, i + PAIR))
         total = sum_squares(x0[1])
         for c in range(CB):
             down(0, c)
             if (c + 1) * IB == LEAD:
                 rms_norm(x0[1], total, gain1, hn[1])
-        for i in range(IB):
-            gated(1, i)
+        for i in range(0, IB, PAIR):
+            gated(1, range(i, i + PAIR))
         total = sum_squares(x1[0])
         for c in range(CB):
             down(1, c)

@@ -35,27 +35,25 @@ def tile_residualbitnettransformer_b_kernel(
     ):
         rd_sb = [held.tile([P, VB, NH], BF16, name=f"rd{half}") for half in range(HALVES)]
         rw_sb = held.tile([P, VB, D], BF16, name="rw")
+        rd_blocks = rd.rearrange("(p k) j -> p k j", k=VB)
+        rw_blocks = resid_w.rearrange("(p k) c -> p k c", k=VB)
 
         def load_rd(half, first, last):
-            rows = rd[first * P : last * P, half * NH : (half + 1) * NH]
-            nc.sync.dma_start(rd_sb[half][:, first:last, :], rows.rearrange("(k p) j -> p k j", p=P))
+            nc.sync.dma_start(rd_sb[half][:, first:last, :], rd_blocks[:, first:last, half * NH : (half + 1) * NH])
 
         emb_sb = [held.tile([P, V], F32, name=f"emb{c}") for c in range(CB)]
         for first, last in zip(GROWING, GROWING[1:]):
             load_rd(0, first, last)
-            rows = resid_w[first * P : last * P, :]
-            nc.scalar.dma_start(rw_sb[:, first:last, :], rows.rearrange("(k p) c -> p k c", p=P))
+            nc.scalar.dma_start(rw_sb[:, first:last, :], rw_blocks[:, first:last, :])
         offsets = held.tile([P, N // 16], U16, name="offsets")
         nc.sync.dma_start(offsets[:], offs)
-        gain1 = held.tile([P, CB], F32, name="gain1")
-        gain2 = held.tile([P, CB], F32, name="gain2")
-        nc.scalar.dma_start(gain1[:], ffn_gain.rearrange("(a p) o -> p (a o)", p=P))
-        nc.scalar.dma_start(gain2[:], norm_gain.rearrange("(a p) o -> p (a o)", p=P))
         for c in range(CB):
             nc.sync.dma_start(emb_sb[c][:], emb[c * P : (c + 1) * P, :])
-            if c % 2 == 1:
-                load_rd(1, c - 1, c + 1)
-        load_rd(1, VB // 2, VB)
+            load_rd(1, c, c + 1)
+        load_rd(1, CB, VB)
+        gain1 = held.tile([P, CB], F32, name="gain1")
+        gain2 = held.tile([P, CB], F32, name="gain2")
+        nc.sync.dma_start(gain1[:], ffn_gain.rearrange("(a p) o -> p (a o)", p=P))
         wg_sb = [held.tile([P, CB, WCOLS], BF16, name=f"wg{w}") for w in range(WLOADS)]
         wu_sb = [held.tile([P, CB, WCOLS], BF16, name=f"wu{w}") for w in range(WLOADS)]
         for w in range(WLOADS):
@@ -68,6 +66,7 @@ def tile_residualbitnettransformer_b_kernel(
             nc.sync.dma_start(wd_sb[w][:], w_down[units, :].rearrange("(i p) c -> p i c", p=P))
         hw_sb = held.tile([P, CB, V], BF16, name="hw")
         nc.sync.dma_start(hw_sb[:], head_w.rearrange("(c p) m -> p c m", p=P))
+        nc.sync.dma_start(gain2[:], norm_gain.rearrange("(a p) o -> p (a o)", p=P))
 
         ones = held.tile([P, P], BF16, name="ones")
         nc.gpsimd.memset(ones[:], 1.0)

@@ -5,6 +5,7 @@ BF16 = mybir.dt.bfloat16
 U16 = mybir.dt.uint16
 ACT = mybir.ActivationFunctionType
 ALU = mybir.AluOpType
+AX = mybir.AxisListType
 
 P = 128
 V, D, HID, N = 1024, 512, 1536, 1024
@@ -20,6 +21,9 @@ CUT = (4, 5)
 PAIR = 2
 WARM = 12
 LEAD = 12
+LONG_LEAD = 24
+BLK = 32
+NB = NH // BLK
 
 FLOPS = 2 * N * (V * D + 2 * D * HID + HID * D + D * V)
 
@@ -73,6 +77,13 @@ def tile_residualbitnettransformer_b_kernel(
         sum_w = ones[:]
         eps = held.tile([P, 1], F32, name="eps")
         nc.vector.memset(eps[:], EPS)
+        fold = held.tile([P, P], BF16, name="fold")
+        nc.gpsimd.memset(fold[:], 0.0)
+        for diagonal in range(1 - P // BLK, P // BLK):
+            nc.gpsimd.affine_select(
+                out=fold[:], in_=fold[:], pattern=[[-1, P]], compare_op=ALU.not_equal, fill=1.0,
+                base=BLK * diagonal, channel_multiplier=1,
+            )
 
         x0 = [[held.tile([P, NH], F32, name=f"x0_{half}_{c}") for c in range(CB)] for half in range(HALVES)]
         x1 = [[held.tile([P, NH], F32, name=f"x1_{half}_{c}") for c in range(CB)] for half in range(HALVES)]
@@ -107,18 +118,38 @@ def tile_residualbitnettransformer_b_kernel(
         def sum_squares(x):
             total = None
             for c in range(CB):
-                sq = work.tile([P, NH], BF16, name="sq")
+                sq = work.tile([P, NH], BF16, name="sq", align_bytes=64)
                 nc.scalar.activation(sq[:], x[c][:], ACT.Square)
                 if c > 0:
                     nc.vector.tensor_tensor(sq[:], sq[:], total[:], ALU.add)
                 total = sq
             return total
 
-        def rms_norm(x, total, gain, dst):
+        def wide_inverse_rms(total):
             ss_ps = acc.tile([P, NH], F32, name="ss_ps", tag="acc")
             nc.tensor.matmul(ss_ps[:], sum_w, total[:], start=True, stop=True)
-            rstd = work.tile([P, NH], F32, name="rstd")
+            rstd = work.tile([P, NH], F32, name="rstd", align_bytes=64)
             nc.scalar.activation(rstd[:], ss_ps[:], ACT.Abs_reciprocal_sqrt, bias=eps[:], scale=1.0 / D)
+            return rstd
+
+        def narrow_inverse_rms(total):
+            flipped = work.tile([P, NH], BF16, name="flipped", align_bytes=64)
+            nc.vector.transpose(flipped[:], total[:])
+            part = work.tile([P, NB], BF16, name="part")
+            with nc.allow_low_precision(reason="part is the moving operand of a bfloat16 matmul, which adds in float32"):
+                nc.vector.tensor_reduce(part[:], flipped[:].rearrange("p (b j) -> p b j", j=BLK), axis=AX.X, op=ALU.add)
+            ss_ps = acc.tile([P, NB], F32, name="ss_ps", tag="acc")
+            nc.tensor.matmul(ss_ps[:], fold[:], part[:], start=True, stop=True)
+            spread = work.tile([P, NH], F32, name="spread", align_bytes=64)
+            nc.scalar.activation(
+                spread[:].rearrange("p (b j) -> p b j", j=BLK), ss_ps[:].unsqueeze(2).to_broadcast([P, NB, BLK]),
+                ACT.Abs_reciprocal_sqrt, bias=eps[:], scale=1.0 / D,
+            )
+            rstd = work.tile([P, NH], F32, name="rstd", align_bytes=64)
+            nc.vector.transpose(rstd[:], spread[:])
+            return rstd
+
+        def rms_norm(x, rstd, gain, dst):
             for c in range(CB):
                 nc.vector.scalar_tensor_tensor(
                     out=dst[c][:], in0=x[c][:], scalar=gain[:, c : c + 1], in1=rstd[:], op0=ALU.mult, op1=ALU.mult
@@ -164,26 +195,26 @@ def tile_residualbitnettransformer_b_kernel(
         embed_end(0, embed_begin(0))
         total = sum_squares(x0[0])
         banks = embed_begin(1)
-        rms_norm(x0[0], total, gain1, hn[0])
+        rms_norm(x0[0], wide_inverse_rms(total), gain1, hn[0])
         embed_end(1, banks)
         for i in range(0, IB, PAIR):
             gated(0, range(i, i + PAIR))
         total = sum_squares(x0[1])
         for c in range(CB):
             down(0, c)
-            if (c + 1) * IB == LEAD:
-                rms_norm(x0[1], total, gain1, hn[1])
+            if (c + 1) * IB == LONG_LEAD:
+                rms_norm(x0[1], narrow_inverse_rms(total), gain1, hn[1])
         for i in range(0, IB, PAIR):
             gated(1, range(i, i + PAIR))
         total = sum_squares(x1[0])
         for c in range(CB):
             down(1, c)
-            if (c + 1) * IB == LEAD:
-                rms_norm(x1[0], total, gain2, yn[0])
+            if (c + 1) * IB == LONG_LEAD:
+                rms_norm(x1[0], narrow_inverse_rms(total), gain2, yn[0])
         total = sum_squares(x1[1])
         for m in range(VB):
             head(0, m)
             if (m + 1) * CB == LEAD:
-                rms_norm(x1[1], total, gain2, yn[1])
+                rms_norm(x1[1], wide_inverse_rms(total), gain2, yn[1])
         for m in range(VB):
             head(1, m)

@@ -177,16 +177,14 @@ def tile_residualbitnettransformer_b_kernel(
                     d_ps[:], wd_sb[i // WB][:, i % WB, c * P : (c + 1) * P], av[half][i][:], start=(i == 0), stop=(i == IB - 1)
                 )
             nc.vector.tensor_tensor(x1[half][c][:], x0[half][c][:], d_ps[:], ALU.add)
+            nc.vector.tensor_scalar_mul(yn[half][c][:], x1[half][c][:], gain2[:, c : c + 1])
 
-        def head(half, m):
+        def head(half, m, rstd):
             l_ps = acc.tile([P, NH], F32, name="l_ps", tag="acc")
             for c in range(CB):
                 nc.tensor.matmul(l_ps[:], hw_sb[:, c, m * P : (m + 1) * P], yn[half][c][:], start=(c == 0), stop=(c == CB - 1))
             l_sb = work.tile([P, NH], F32, name="l_sb")
-            if m % 2 == 0:
-                nc.scalar.copy(l_sb[:], l_ps[:])
-            else:
-                nc.vector.tensor_copy(l_sb[:], l_ps[:])
+            nc.vector.tensor_tensor(l_sb[:], l_ps[:], rstd[:], ALU.mult)
             nc.sync.dma_start(out[m * P : (m + 1) * P, half * NH : (half + 1) * NH], l_sb[:])
 
         warm_ps = acc.tile([P, P], F32, name="warm_ps", tag="acc")
@@ -210,11 +208,11 @@ def tile_residualbitnettransformer_b_kernel(
         for c in range(CB):
             down(1, c)
             if (c + 1) * IB == LONG_LEAD:
-                rms_norm(x1[0], narrow_inverse_rms(total), gain2, yn[0])
+                rstd_0 = narrow_inverse_rms(total)
         total = sum_squares(x1[1])
         for m in range(VB):
-            head(0, m)
-            if (m + 1) * CB == LEAD:
-                rms_norm(x1[1], wide_inverse_rms(total), gain2, yn[1])
+            head(0, m, rstd_0)
+            if (m + 1) * CB == LONG_LEAD:
+                rstd_1 = narrow_inverse_rms(total)
         for m in range(VB):
-            head(1, m)
+            head(1, m, rstd_1)

@@ -179,13 +179,17 @@ def tile_residualbitnettransformer_b_kernel(
             nc.vector.tensor_tensor(x1[half][c][:], x0[half][c][:], d_ps[:], ALU.add)
             nc.vector.tensor_scalar_mul(yn[half][c][:], x1[half][c][:], gain2[:, c : c + 1])
 
-        def head(half, m, rstd):
+        def head(half, m, rstd, pieces=1):
             l_ps = acc.tile([P, NH], F32, name="l_ps", tag="acc")
             for c in range(CB):
                 nc.tensor.matmul(l_ps[:], hw_sb[:, c, m * P : (m + 1) * P], yn[half][c][:], start=(c == 0), stop=(c == CB - 1))
             l_sb = work.tile([P, NH], F32, name="l_sb")
-            nc.vector.tensor_tensor(l_sb[:], l_ps[:], rstd[:], ALU.mult)
-            nc.sync.dma_start(out[m * P : (m + 1) * P, half * NH : (half + 1) * NH], l_sb[:])
+            width = NH // pieces
+            for piece in range(pieces):
+                cols = slice(piece * width, (piece + 1) * width)
+                nc.vector.tensor_tensor(l_sb[:, cols], l_ps[:, cols], rstd[:, cols], ALU.mult)
+                queue = nc.sync if (m + piece) % 2 == 0 else nc.scalar
+                queue.dma_start(out[m * P : (m + 1) * P, half * NH + cols.start : half * NH + cols.stop], l_sb[:, cols])
 
         warm_ps = acc.tile([P, P], F32, name="warm_ps", tag="acc")
         for r in range(WARM):
@@ -215,4 +219,4 @@ def tile_residualbitnettransformer_b_kernel(
             if (m + 1) * CB == LONG_LEAD:
                 rstd_1 = narrow_inverse_rms(total)
         for m in range(VB):
-            head(1, m, rstd_1)
+            head(1, m, rstd_1, pieces=2 if m == VB - 1 else 1)

import concourse.mybir as mybir

F32 = mybir.dt.float32
BF16 = mybir.dt.bfloat16
U16 = mybir.dt.uint16
ACT = mybir.ActivationFunctionType
ALU = mybir.AluOpType
AX = mybir.AxisListType

P = 128
V, D, HID, N = 1024, 512, 1536, 1024
EPS = 1e-6
NH = 512
HALVES = N // NH
VB, CB, IB = V // P, D // P, HID // P
WCOLS = 512
WB = WCOLS // P
WLOADS = HID // WCOLS
GROWING = (0, 1, 2, 4, 8)
CUT = (4, 5)
PAIR = 2
WARM = 12
LEAD = 12
LONG_LEAD = 24
BLK = 32
NB = NH // BLK

FLOPS = 2 * N * (V * D + 2 * D * HID + HID * D + D * V)


def tile_residualbitnettransformer_b_kernel(
    tc, emb, rd, resid_w, ffn_gain, w_gate, w_up, w_down, norm_gain, head_w, offs, out
):
    nc = tc.nc
    with (
        tc.tile_pool(name="held", bufs=1) as held,
        tc.tile_pool(name="work", bufs=4) as work,
        tc.psum_pool(name="acc", bufs=8) as acc,
    ):
        rd_sb = [held.tile([P, VB, NH], BF16, name=f"rd{half}") for half in range(HALVES)]
        rw_sb = held.tile([P, VB, D], BF16, name="rw")
        rd_blocks = rd.rearrange("(p k) j -> p k j", k=VB)
        rw_blocks = resid_w.rearrange("(p k) c -> p k c", k=VB)

        def load_rd(half, first, last):
            nc.sync.dma_start(rd_sb[half][:, first:last, :], rd_blocks[:, first:last, half * NH : (half + 1) * NH])

        emb_sb = [held.tile([P, V], F32, name=f"emb{c}") for c in range(CB)]
        for first, last in zip(GROWING, GROWING[1:]):
            load_rd(0, first, last)
            nc.scalar.dma_start(rw_sb[:, first:last, :], rw_blocks[:, first:last, :])
        offsets = held.tile([P, N // 16], U16, name="offsets")
        nc.sync.dma_start(offsets[:], offs)
        for c in range(CB):
            nc.sync.dma_start(emb_sb[c][:], emb[c * P : (c + 1) * P, :])
            load_rd(1, c, c + 1)
        load_rd(1, CB, VB)
        gain1 = held.tile([P, CB], F32, name="gain1")
        gain2 = held.tile([P, CB], F32, name="gain2")
        nc.sync.dma_start(gain1[:], ffn_gain.rearrange("(a p) o -> p (a o)", p=P))
        wg_sb = [held.tile([P, CB, WCOLS], BF16, name=f"wg{w}") for w in range(WLOADS)]
        wu_sb = [held.tile([P, CB, WCOLS], BF16, name=f"wu{w}") for w in range(WLOADS)]
        for w in range(WLOADS):
            units = slice(w * WCOLS, (w + 1) * WCOLS)
            nc.sync.dma_start(wg_sb[w][:], w_gate[:, units].rearrange("(c p) i -> p c i", p=P))
            nc.sync.dma_start(wu_sb[w][:], w_up[:, units].rearrange("(c p) i -> p c i", p=P))
        wd_sb = [held.tile([P, WB, D], BF16, name=f"wd{w}") for w in range(WLOADS)]
        for w in range(WLOADS):
            units = slice(w * WCOLS, (w + 1) * WCOLS)
            nc.sync.dma_start(wd_sb[w][:], w_down[units, :].rearrange("(i p) c -> p i c", p=P))
        hw_sb = held.tile([P, CB, V], BF16, name="hw")
        nc.sync.dma_start(hw_sb[:], head_w.rearrange("(c p) m -> p c m", p=P))
        nc.sync.dma_start(gain2[:], norm_gain.rearrange("(a p) o -> p (a o)", p=P))

        ones = held.tile([P, P], BF16, name="ones")
        nc.gpsimd.memset(ones[:], 1.0)
        sum_w = ones[:]
        eps = held.tile([P, 1], F32, name="eps")
        nc.vector.memset(eps[:], EPS)
        fold = held.tile([P, P], BF16, name="fold")
        nc.gpsimd.memset(fold[:], 0.0)
        for diagonal in range(1 - P // BLK, P // BLK):
            nc.gpsimd.affine_select(
                out=fold[:], in_=fold[:], pattern=[[-1, P]], compare_op=ALU.not_equal, fill=1.0,
                base=BLK * diagonal, channel_multiplier=1,
            )

        x0 = [[held.tile([P, NH], F32, name=f"x0_{half}_{c}") for c in range(CB)] for half in range(HALVES)]
        x1 = [[held.tile([P, NH], F32, name=f"x1_{half}_{c}") for c in range(CB)] for half in range(HALVES)]
        hn = [[held.tile([P, NH], BF16, name=f"hn_{half}_{c}") for c in range(CB)] for half in range(HALVES)]
        yn = [[held.tile([P, NH], BF16, name=f"yn_{half}_{c}") for c in range(CB)] for half in range(HALVES)]
        av = [[held.tile([P, NH], BF16, name=f"av_{half}_{i}") for i in range(IB)] for half in range(HALVES)]

        def project(bank, half, k, c):
            nc.tensor.matmul(
                bank[:], rw_sb[:, k, c * P : (c + 1) * P], rd_sb[half][:, k, :], start=(k == 0), stop=(k == VB - 1)
            )

        def embed_begin(half):
            banks = [acc.tile([P, NH], F32, name=f"p_ps{c}", tag="acc") for c in range(CB)]
            for k in range(CUT[half]):
                for c in range(CB):
                    project(banks[c], half, k, c)
            return banks

        def embed_end(half, banks):
            for c in range(CB):
                for k in range(CUT[half], VB):
                    project(banks[c], half, k, c)
                look_up(banks[c], half, c)

        def look_up(bank, half, c):
            p_sb = work.tile([P, NH], F32, name="p_sb")
            nc.scalar.copy(p_sb[:], bank[:])
            picked = emb_sb[c][:].indirect(offsets[:, half * (NH // 16) : (half + 1) * (NH // 16)])
            nc.vector.tensor_tensor(x0[half][c][:], picked, p_sb[:], ALU.add)

        def sum_squares(x):
            total = None
            for c in range(CB):
                sq = work.tile([P, NH], BF16, name="sq", align_bytes=64)
                nc.scalar.activation(sq[:], x[c][:], ACT.Square)
                if c > 0:
                    nc.vector.tensor_tensor(sq[:], sq[:], total[:], ALU.add)
                total = sq
            return total

        def wide_inverse_rms(total):
            ss_ps = acc.tile([P, NH], F32, name="ss_ps", tag="acc")
            nc.tensor.matmul(ss_ps[:], sum_w, total[:], start=True, stop=True)
            rstd = work.tile([P, NH], F32, name="rstd", align_bytes=64)
            nc.scalar.activation(rstd[:], ss_ps[:], ACT.Abs_reciprocal_sqrt, bias=eps[:], scale=1.0 / D)
            return rstd

        def narrow_inverse_rms(total):
            flipped = work.tile([P, NH], BF16, name="flipped", align_bytes=64)
            nc.vector.transpose(flipped[:], total[:])
            part = work.tile([P, NB], BF16, name="part")
            with nc.allow_low_precision(reason="part is the moving operand of a bfloat16 matmul, which adds in float32"):
                nc.vector.tensor_reduce(part[:], flipped[:].rearrange("p (b j) -> p b j", j=BLK), axis=AX.X, op=ALU.add)
            ss_ps = acc.tile([P, NB], F32, name="ss_ps", tag="acc")
            nc.tensor.matmul(ss_ps[:], fold[:], part[:], start=True, stop=True)
            spread = work.tile([P, NH], F32, name="spread", align_bytes=64)
            nc.scalar.activation(
                spread[:].rearrange("p (b j) -> p b j", j=BLK), ss_ps[:].unsqueeze(2).to_broadcast([P, NB, BLK]),
                ACT.Abs_reciprocal_sqrt, bias=eps[:], scale=1.0 / D,
            )
            rstd = work.tile([P, NH], F32, name="rstd", align_bytes=64)
            nc.vector.transpose(rstd[:], spread[:])
            return rstd

        def rms_norm(x, rstd, gain, dst):
            for c in range(CB):
                nc.vector.scalar_tensor_tensor(
                    out=dst[c][:], in0=x[c][:], scalar=gain[:, c : c + 1], in1=rstd[:], op0=ALU.mult, op1=ALU.mult
                )

        def gated(half, blocks):
            g_ps = {i: acc.tile([P, NH], F32, name="g_ps", tag="acc") for i in blocks}
            u_ps = {i: acc.tile([P, NH], F32, name="u_ps", tag="acc") for i in blocks}
            for c in range(CB):
                for banks, w_sb in ((g_ps, wg_sb), (u_ps, wu_sb)):
                    for i in blocks:
                        cols = slice((i % WB) * P, (i % WB + 1) * P)
                        nc.tensor.matmul(
                            banks[i][:], w_sb[i // WB][:, c, cols], hn[half][c][:], start=(c == 0), stop=(c == CB - 1)
                        )
            for i in blocks:
                sil = work.tile([P, NH], F32, name="sil")
                nc.scalar.activation(sil[:], g_ps[i][:], ACT.Silu)
                nc.vector.tensor_tensor(av[half][i][:], sil[:], u_ps[i][:], ALU.mult)

        def down(half, c):
            d_ps = acc.tile([P, NH], F32, name="d_ps", tag="acc")
            for i in range(IB):
                nc.tensor.matmul(
                    d_ps[:], wd_sb[i // WB][:, i % WB, c * P : (c + 1) * P], av[half][i][:], start=(i == 0), stop=(i == IB - 1)
                )
            nc.vector.tensor_tensor(x1[half][c][:], x0[half][c][:], d_ps[:], ALU.add)
            nc.vector.tensor_scalar_mul(yn[half][c][:], x1[half][c][:], gain2[:, c : c + 1])

        def head(half, m, rstd, pieces=1):
            l_ps = acc.tile([P, NH], F32, name="l_ps", tag="acc")
            for c in range(CB):
                nc.tensor.matmul(l_ps[:], hw_sb[:, c, m * P : (m + 1) * P], yn[half][c][:], start=(c == 0), stop=(c == CB - 1))
            l_sb = work.tile([P, NH], F32, name="l_sb")
            width = NH // pieces
            for piece in range(pieces):
                cols = slice(piece * width, (piece + 1) * width)
                nc.vector.tensor_tensor(l_sb[:, cols], l_ps[:, cols], rstd[:, cols], ALU.mult)
                queue = nc.sync if (m + piece) % 2 == 0 else nc.scalar
                queue.dma_start(out[m * P : (m + 1) * P, half * NH + cols.start : half * NH + cols.stop], l_sb[:, cols])

        warm_ps = acc.tile([P, P], F32, name="warm_ps", tag="acc")
        for r in range(WARM):
            nc.tensor.matmul(warm_ps[:], sum_w, ones[:], start=True, stop=True)
        embed_end(0, embed_begin(0))
        total = sum_squares(x0[0])
        banks = embed_begin(1)
        rms_norm(x0[0], wide_inverse_rms(total), gain1, hn[0])
        embed_end(1, banks)
        for i in range(0, IB, PAIR):
            gated(0, range(i, i + PAIR))
        total = sum_squares(x0[1])
        for c in range(CB):
            down(0, c)
            if (c + 1) * IB == LONG_LEAD:
                rms_norm(x0[1], narrow_inverse_rms(total), gain1, hn[1])
        for i in range(0, IB, PAIR):
            gated(1, range(i, i + PAIR))
        total = sum_squares(x1[0])
        for c in range(CB):
            down(1, c)
            if (c + 1) * IB == LONG_LEAD:
                rstd_0 = narrow_inverse_rms(total)
        total = sum_squares(x1[1])
        for m in range(VB):
            head(0, m, rstd_0)
            if (m + 1) * CB == LONG_LEAD:
                rstd_1 = narrow_inverse_rms(total)
        for m in range(VB):
            head(1, m, rstd_1, pieces=2 if m == VB - 1 else 1)
